import numpy as np
import ml_dtypes


def mxq(x, axis, fmt="e4m3"):
    dtype, down = {"e4m3": (ml_dtypes.float8_e4m3fn, 7), "e5m2": (ml_dtypes.float8_e5m2, 14)}[fmt]
    v = np.moveaxis(np.asarray(x, np.float32).astype(ml_dtypes.bfloat16).astype(np.float64), axis, -1)
    blocks = v.reshape(v.shape[:-1] + (-1, 32))
    amax = np.abs(blocks).max(-1, keepdims=True)
    byte = np.maximum(np.where(amax > 0, np.frexp(amax)[1] - 1 + 127, 0) - down, 1)
    scale = np.exp2(byte - 127.0)
    codes = (blocks / scale).astype(np.float32).astype(dtype).astype(np.float64)
    return np.moveaxis((codes * scale).reshape(v.shape), -1, axis)


WIDE = False


def mx_kscale(k):
    if not WIDE:
        return np.ones(k)
    levels = np.array([10, -10, 5, -5, 0])
    if k % 512:
        return np.exp2(np.random.permutation(np.resize(levels, k // 32))).repeat(32)
    a = np.empty((k // 512, 16))
    for p in range(k // 512):
        a[p, :8] = np.random.permutation(np.resize(levels, 8))
        for g in range(8):
            far = levels[np.abs(levels - a[p, g]) >= 10]
            a[p, g + 8] = far[np.random.randint(len(far))]
    return np.exp2(a.ravel()).repeat(32)


BF16 = ml_dtypes.bfloat16


def bf(x):
    return np.asarray(x, np.float32).astype(BF16)


def f64(x):
    return np.asarray(x).astype(np.float64)


B, C, IN, H, ND, NG, NL = 32, 128, 512, 256, 2, 4, 2
N = B * C
USED = [0, 2, 3]


def sigmoid(v):
    return 1.0 / (1.0 + np.exp(-v))


def cell(inq, w, b1, b2):
    wu = w.reshape(NG, H, -1)[USED].reshape(len(USED) * H, -1)
    gates = (inq @ mxq(wu.T, 0, "e4m3")) + b1.reshape(NG, H)[USED].reshape(-1) + b2.reshape(NG, H)[USED].reshape(-1)
    i, g, o = np.split(gates, len(USED), axis=-1)
    c = sigmoid(i) * np.tanh(g)
    return sigmoid(o) * np.tanh(c)


def setup_inputs():
    s = mx_kscale(IN)
    return {"x": bf(np.random.standard_normal((B, C, IN)) * s),
            "w_ih": bf(np.random.standard_normal((ND, NG * H, IN)) * 1.5 / np.sqrt(IN) / s),
            "b_ih": bf(np.random.standard_normal((ND, NG * H)) * 0.3),
            "b_hh": bf(np.random.standard_normal((ND, NG * H)) * 0.3)}


def reference(x, w_ih, b_ih, b_hh):
    xq = mxq(f64(x).reshape(N, IN), 1, "e4m3")
    w, b1, b2 = f64(w_ih), f64(b_ih), f64(b_hh)
    return np.concatenate([cell(xq, w[d], b1[d], b2[d]) for d in range(ND)], axis=-1)

@@ -1,0 +1,269 @@
+from contextlib import ExitStack
+
+import concourse.masks as masks
+import concourse.mybir as mybir
+
+F32 = mybir.dt.float32
+BF16 = mybir.dt.bfloat16
+U32 = mybir.dt.uint32
+U8 = mybir.dt.uint8
+FP8X4 = mybir.dt.float8_e4m3fn_x4
+ACT = mybir.ActivationFunctionType
+ALU = mybir.AluOpType
+
+P = 128
+ROWS = 4096
+K = 512
+H = 256
+ND = 2
+CHUNK = 512
+NCHUNK = ROWS // CHUNK
+RT = CHUNK // P
+NQ = 4
+GATE_I, GATE_G, GATE_O = 0, 2, 3
+PATTERN = (("o", 0), ("c", 0), ("o", 1), ("c", 1), ("o", 2), ("c", 2), ("o", 3), ("c", 3), ("x", 0), ("x", 1))
+RA, RV = 5, 3
+LAST_PIECES = 1
+NWARM = 4
+TAIL = (("o", 0), ("o", 1), ("o", 2), ("c", 0), ("c", 1), ("o", 3), ("c", 2), ("c", 3))
+DEPTH = {"s_i": 2, "t_g": 2, "cell": 3, "s_o": 3, "t_c": 3, "hid": 3}
+
+FLOPS = 2 * ROWS * (3 * H * ND) * K
+BYTES = ROWS * K * 2 + ND * 3 * H * K * 2 + 2 * ND * 3 * H * 2 + ROWS * ND * H * 4
+
+
+def tile_lstmnetwork_pa_t_kernel(tc, x, w_ih, b_ih, b_hh, out):
+    nc = tc.nc
+    xv = x.flatten_outer_dims().rearrange("(c r t) k -> c r (t k)", r=P, t=RT)
+    outv = out.rearrange("(c r t) n -> c r (t n)", r=P, t=RT)
+
+    with ExitStack() as ctx:
+        ctx.enter_context(tc.manual_schedule())
+        const = ctx.enter_context(tc.tile_pool(name="const", bufs=1))
+        xin = ctx.enter_context(tc.tile_pool(name="xin", bufs=1))
+        stage = ctx.enter_context(tc.tile_pool(name="stage", bufs=2))
+        xq = ctx.enter_context(tc.tile_pool(name="xq", bufs=3))
+        work = ctx.enter_context(tc.tile_pool(name="work", bufs=2))
+        ring_a = ctx.enter_context(tc.psum_pool(name="ring_a", bufs=RA))
+        ring_v = ctx.enter_context(tc.psum_pool(name="ring_v", bufs=RV))
+
+        bi = const.tile([16, P], BF16, name="bi")
+        bh = const.tile([16, P], BF16, name="bh")
+        nc.scalar.dma_start(out=bi[:], in_=b_ih.rearrange("d (g p) -> (d g) p", p=P))
+        nc.scalar.dma_start(out=bh[:], in_=b_hh.rearrange("d (g p) -> (d g) p", p=P))
+        zeros = const.tile([P, 512], BF16, name="zeros")
+        nc.vector.memset(zeros[:], 0.0)
+        spin = ring_a.tile([P, 512], F32, name="spin", tag="a")
+        for i in range(NWARM):
+            nc.tensor.matmul(out=spin[:], lhsT=zeros[:, 0:P], rhs=zeros[:], start=True, stop=True)
+        warm = const.tile([P, 1], F32, name="warm")
+        nc.vector.memset(warm[:], 0.0)
+        nc.scalar.activation(out=warm[:], in_=warm[:], func=ACT.Sigmoid)
+        ident = const.tile([P, P], F32, name="ident")
+        masks.make_identity(nc, ident[:])
+        bsum = const.tile([P, P], F32, name="bsum")
+        nc.vector.memset(bsum[:], 0.0)
+
+        w_raw = {}
+        x_raw = {}
+
+        def load_w(gate, d):
+            t = const.tile([P, 2 * K], BF16, name="wraw%d_%d" % (gate, d))
+            nc.sync.dma_start(
+                out=t[:].rearrange("p (h k) -> p h k", h=2),
+                in_=w_ih[d, gate * H : (gate + 1) * H, :].rearrange("(h p) k -> p h k", p=P),
+            )
+            w_raw[(gate, d)] = t
+
+        def load_x(c, pieces):
+            t = xin.tile([P, RT * K], BF16, name="xraw%d" % c)
+            step = RT * K // pieces
+            for i in range(pieces):
+                nc.sync.dma_start(out=t[:, i * step : (i + 1) * step], in_=xv[c][:, i * step : (i + 1) * step])
+            x_raw[c] = t
+
+        load_x(0, 2)
+        load_w(GATE_I, 0)
+        load_w(GATE_I, 1)
+        load_w(GATE_G, 0)
+        load_w(GATE_G, 1)
+        load_w(GATE_O, 0)
+        load_w(GATE_O, 1)
+        for c in range(1, NCHUNK):
+            load_x(c, 1)
+
+        def turn(raw, first):
+            raw32 = raw[:].bitcast(F32)
+            bank = ring_v.tile([P, 512], F32, name="turn", tag="v")
+            for j in range(2):
+                for u in range(2):
+                    nc.tensor.transpose(
+                        bank[:, (2 * j + u) * P : (2 * j + u + 1) * P],
+                        raw32[:, (first + j) * 256 + u : (first + j + 1) * 256 : 2],
+                        ident[:],
+                    )
+            return bank
+
+        def regroup(engine_copy, bank, grouped, pair):
+            g32 = grouped[:].bitcast(F32)
+            engine_copy(
+                out=g32[:, pair * 512 : (pair + 1) * 512].rearrange("p (j r u) -> p j r u", j=2, u=2),
+                in_=bank[:].rearrange("p (j u r) -> p j r u", j=2, u=2),
+            )
+
+        w_grp = {}
+        w_codes = {}
+        w_scales = {}
+
+        def turn_w(gate, d, engine_copy):
+            grouped = stage.tile([P, 4 * 2 * P], BF16, name="wgrp", align_bytes=64, bufs=3)
+            regroup(engine_copy, turn(w_raw[(gate, d)], 0), grouped, 0)
+            w_grp[(gate, d)] = grouped
+
+        def quant_w(gate, d):
+            codes = const.tile([P, 2 * P], U32, name="wc%d_%d" % (gate, d), align_bytes=64)
+            scales = const.tile([P, 2 * P], U8, name="ws%d_%d" % (gate, d), align_bytes=64)
+            nc.vector.quantize_mx(out=codes[:].bitcast(FP8X4), scales=scales[:], in_=w_grp[(gate, d)][:])
+            w_codes[(gate, d)] = codes
+            w_scales[(gate, d)] = scales
+
+        x_grp = {}
+        x_codes = {}
+        x_scales = {}
+
+        def turn_x(c, pair, engine_copy):
+            if pair == 0:
+                x_grp[c] = stage.tile([P, 4 * CHUNK], BF16, name="xgrp", align_bytes=64)
+            regroup(engine_copy, turn(x_raw[c], 2 * pair), x_grp[c], pair)
+
+        def quant_x(c, lo, hi):
+            if c not in x_codes:
+                x_codes[c] = xq.tile([P, CHUNK], U32, name="xc", align_bytes=64)
+                x_scales[c] = xq.tile([P, CHUNK], U8, name="xs", align_bytes=64)
+            nc.vector.quantize_mx(
+                out=x_codes[c][:, lo:hi].bitcast(FP8X4), scales=x_scales[c][:, lo:hi], in_=x_grp[c][:, 4 * lo : 4 * hi]
+            )
+
+        bias = const.tile([P, 16], F32, name="bias")
+        tiles = {}
+
+        def buf(c, name):
+            if (c, name) not in tiles:
+                tiles[(c, name)] = work.tile([P, NQ * CHUNK], F32, name=name, bufs=DEPTH[name])
+            return tiles[(c, name)]
+
+        def gate_act(c, gate, q, func, name, lo=0, hi=CHUNK):
+            d, h = divmod(q, 2)
+            acc = ring_a.tile([P, hi - lo], F32, name="acc", tag="a")
+            nc.tensor.matmul_mx(
+                out=acc[:],
+                lhsT=w_codes[(gate, d)][:, h * P : (h + 1) * P].bitcast(FP8X4),
+                lhsT_scale=w_scales[(gate, d)][:, h * P : (h + 1) * P],
+                rhs=x_codes[c][:, lo:hi].bitcast(FP8X4),
+                rhs_scale=x_scales[c][:, lo:hi],
+                start=True,
+                stop=True,
+            )
+            col = d * 8 + gate * 2 + h
+            nc.scalar.activation(
+                out=buf(c, name)[:, q * CHUNK + lo : q * CHUNK + hi],
+                in_=acc[:],
+                func=func,
+                bias=bias[:, col : col + 1],
+                scale=1.0,
+            )
+
+        def cell_product(c, q, engine):
+            sl = slice(q * CHUNK, (q + 1) * CHUNK)
+            engine.tensor_tensor(
+                out=buf(c, "cell")[:, sl], in0=buf(c, "s_i")[:, sl], in1=buf(c, "t_g")[:, sl], op=ALU.mult
+            )
+
+        def turn_back(pool, tag, src, t):
+            bank = pool.tile([P, 512], F32, name="back_" + tag, tag=tag)
+            for q in range(NQ):
+                nc.tensor.transpose(
+                    bank[:, q * P : (q + 1) * P], src[:, q * CHUNK + t * P : q * CHUNK + (t + 1) * P], ident[:]
+                )
+            return bank
+
+        def cell_tanh(c, t, pieces=1):
+            bank = turn_back(ring_a, "a", buf(c, "cell"), t)
+            w = 512 // pieces
+            for i in range(pieces):
+                nc.scalar.activation(
+                    out=buf(c, "t_c")[:, t * 512 + i * w : t * 512 + (i + 1) * w],
+                    in_=bank[:, i * w : (i + 1) * w],
+                    func=ACT.Tanh,
+                )
+
+        def hidden(c, t, pieces=1):
+            bank = turn_back(ring_v, "v", buf(c, "s_o"), t)
+            w = 512 // pieces
+            for i in range(pieces):
+                sl = slice(t * 512 + i * w, t * 512 + (i + 1) * w)
+                nc.vector.tensor_tensor(
+                    out=buf(c, "hid")[:, sl], in0=bank[:, i * w : (i + 1) * w], in1=buf(c, "t_c")[:, sl], op=ALU.mult
+                )
+                if c == NCHUNK - 1 and t == RT - 1:
+                    nc.sync.dma_start(out=outv[c][:, sl], in_=buf(c, "hid")[:, sl])
+
+        nc.vector.tensor_tensor(out=bsum[0:16, :], in0=bi[:], in1=bh[:], op=ALU.add)
+        turn_x(0, 0, nc.vector.tensor_copy)
+        turn_x(0, 1, nc.vector.tensor_copy)
+        turn_w(GATE_I, 0, nc.scalar.copy)
+        turn_w(GATE_I, 1, nc.scalar.copy)
+        quant_x(0, 0, CHUNK)
+        quant_w(GATE_I, 0)
+        bias_ps = ring_v.tile([P, 512], F32, name="bias_ps", tag="v")
+        nc.tensor.transpose(bias_ps[:, 0:P], bsum[:], ident[:])
+        nc.vector.tensor_copy(out=bias[:], in_=bias_ps[:, 0:16])
+        quant_w(GATE_I, 1)
+        turn_w(GATE_G, 0, nc.vector.tensor_copy)
+        turn_w(GATE_G, 1, nc.vector.tensor_copy)
+        for q in range(NQ):
+            gate_act(0, GATE_I, q, ACT.Sigmoid, "s_i")
+        quant_w(GATE_G, 0)
+        quant_w(GATE_G, 1)
+        turn_w(GATE_O, 0, nc.vector.tensor_copy)
+        turn_w(GATE_O, 1, nc.vector.tensor_copy)
+        quant_w(GATE_O, 0)
+        quant_w(GATE_O, 1)
+
+        def store(c, t0, t1):
+            nc.sync.dma_start(out=outv[c][:, t0 * 512 : t1 * 512], in_=buf(c, "hid")[:, t0 * 512 : t1 * 512])
+
+        for c in range(NCHUNK):
+            last = c == NCHUNK - 1
+            if c > 0:
+                for q in range(NQ):
+                    gate_act(c, GATE_I, q, ACT.Sigmoid, "s_i")
+            for q in range(NQ):
+                gate_act(c, GATE_G, q, ACT.Tanh, "t_g")
+            for kind, t in PATTERN:
+                if kind == "c" and c >= 1:
+                    cell_tanh(c - 1, t)
+                if kind == "o" and c >= 2:
+                    hidden(c - 2, t)
+                if kind == "x" and not last:
+                    turn_x(c + 1, t, nc.vector.tensor_copy)
+            if not last:
+                quant_x(c + 1, 0, CHUNK)
+            if c >= 2:
+                store(c - 2, 0, RT)
+            for q in range(NQ):
+                cell_product(c, q, nc.vector)
+            for q in range(NQ):
+                gate_act(c, GATE_O, q, ACT.Sigmoid, "s_o")
+        c = NCHUNK - 1
+        for kind, t in TAIL:
+            if kind == "o":
+                hidden(c - 1, t)
+                if t % 2 == 1:
+                    store(c - 1, t - 1, t + 1)
+            else:
+                cell_tanh(c, t, LAST_PIECES if t == RT - 1 else 1)
+        for t in range(RT - 1):
+            hidden(c, t)
+            store(c, t, t + 1)
+        hidden(c, RT - 1, LAST_PIECES)

@@ -21,11 +21,9 @@ NCHUNK = ROWS // CHUNK
 RT = CHUNK // P
 NQ = 4
 GATE_I, GATE_G, GATE_O = 0, 2, 3
-PATTERN = (("o", 0), ("c", 0), ("o", 1), ("c", 1), ("o", 2), ("c", 2), ("o", 3), ("c", 3), ("x", 0), ("x", 1))
 RA, RV = 5, 3
-LAST_PIECES = 1
+LAST_PIECES = 2
 NWARM = 4
-TAIL = (("o", 0), ("o", 1), ("o", 2), ("c", 0), ("c", 1), ("o", 3), ("c", 2), ("c", 3))
 DEPTH = {"s_i": 2, "t_g": 2, "cell": 3, "s_o": 3, "t_c": 3, "hid": 3}
 
 FLOPS = 2 * ROWS * (3 * H * ND) * K
@@ -238,31 +236,34 @@ def tile_lstmnetwork_pa_t_kernel(tc, x, w_ih, b_ih, b_hh, out):
             if c > 0:
                 for q in range(NQ):
                     gate_act(c, GATE_I, q, ACT.Sigmoid, "s_i")
-            for q in range(NQ):
-                gate_act(c, GATE_G, q, ACT.Tanh, "t_g")
-            for kind, t in PATTERN:
-                if kind == "c" and c >= 1:
-                    cell_tanh(c - 1, t)
-                if kind == "o" and c >= 2:
-                    hidden(c - 2, t)
-                if kind == "x" and not last:
-                    turn_x(c + 1, t, nc.vector.tensor_copy)
+            if c >= 2:
+                hidden(c - 2, RT - 1)
+                store(c - 2, 0, RT)
+            if c == 0:
+                for q in range(NQ):
+                    gate_act(c, GATE_G, q, ACT.Tanh, "t_g")
+            if not last:
+                for pair in range(2):
+                    turn_x(c + 1, pair, nc.vector.tensor_copy)
+            if c > 0:
+                for q in range(NQ):
+                    gate_act(c, GATE_G, q, ACT.Tanh, "t_g")
             if not last:
                 quant_x(c + 1, 0, CHUNK)
-            if c >= 2:
-                store(c - 2, 0, RT)
             for q in range(NQ):
                 cell_product(c, q, nc.vector)
+            if c >= 1:
+                for t in range(RT):
+                    cell_tanh(c - 1, t)
+                    if t < RT - 1:
+                        hidden(c - 1, t)
             for q in range(NQ):
                 gate_act(c, GATE_O, q, ACT.Sigmoid, "s_o")
         c = NCHUNK - 1
-        for kind, t in TAIL:
-            if kind == "o":
-                hidden(c - 1, t)
-                if t % 2 == 1:
-                    store(c - 1, t - 1, t + 1)
-            else:
-                cell_tanh(c, t, LAST_PIECES if t == RT - 1 else 1)
+        hidden(c - 1, RT - 1)
+        store(c - 1, 0, RT)
+        for t in range(RT):
+            cell_tanh(c, t, LAST_PIECES if t == RT - 1 else 1)
         for t in range(RT - 1):
             hidden(c, t)
             store(c, t, t + 1)

@@ -23,7 +23,7 @@ NQ = 4
 GATE_I, GATE_G, GATE_O = 0, 2, 3
 RA, RV = 5, 3
 LAST_PIECES = 2
-NWARM = 4
+NWARM = 3
 DEPTH = {"s_i": 2, "t_g": 2, "cell": 3, "s_o": 3, "t_c": 3, "hid": 3}
 
 FLOPS = 2 * ROWS * (3 * H * ND) * K
@@ -73,26 +73,26 @@ def tile_lstmnetwork_pa_t_kernel(tc, x, w_ih, b_ih, b_hh, out):
             )
             w_raw[(gate, d)] = t
 
-        def load_x(c, pieces):
-            t = xin.tile([P, RT * K], BF16, name="xraw%d" % c)
-            step = RT * K // pieces
-            for i in range(pieces):
-                nc.sync.dma_start(out=t[:, i * step : (i + 1) * step], in_=xv[c][:, i * step : (i + 1) * step])
-            x_raw[c] = t
+        def load_x(c):
+            x_raw[c] = xin.tile([P, RT * K], BF16, name="xraw%d" % c)
+            nc.sync.dma_start(out=x_raw[c][:], in_=xv[c])
 
-        load_x(0, 2)
+        x_raw[0] = xin.tile([P, RT * K], BF16, name="xraw0")
+        half = RT * K // 2
+        nc.sync.dma_start(out=x_raw[0][:, 0:half], in_=xv[0][:, 0:half])
         load_w(GATE_I, 0)
         load_w(GATE_I, 1)
+        nc.sync.dma_start(out=x_raw[0][:, half : 2 * half], in_=xv[0][:, half : 2 * half])
         load_w(GATE_G, 0)
         load_w(GATE_G, 1)
         load_w(GATE_O, 0)
         load_w(GATE_O, 1)
         for c in range(1, NCHUNK):
-            load_x(c, 1)
+            load_x(c)
 
-        def turn(raw, first):
+        def turn(raw, first, pool=ring_v, tag="v"):
             raw32 = raw[:].bitcast(F32)
-            bank = ring_v.tile([P, 512], F32, name="turn", tag="v")
+            bank = pool.tile([P, 512], F32, name="turn_" + tag, tag=tag)
             for j in range(2):
                 for u in range(2):
                     nc.tensor.transpose(
@@ -113,10 +113,14 @@ def tile_lstmnetwork_pa_t_kernel(tc, x, w_ih, b_ih, b_hh, out):
         w_codes = {}
         w_scales = {}
 
-        def turn_w(gate, d, engine_copy):
-            grouped = stage.tile([P, 4 * 2 * P], BF16, name="wgrp", align_bytes=64, bufs=3)
-            regroup(engine_copy, turn(w_raw[(gate, d)], 0), grouped, 0)
-            w_grp[(gate, d)] = grouped
+        w_bank = {}
+
+        def turn_w(gate, d, pool=ring_v, tag="v"):
+            w_bank[(gate, d)] = turn(w_raw[(gate, d)], 0, pool, tag)
+
+        def group_w(gate, d, engine_copy):
+            w_grp[(gate, d)] = stage.tile([P, 4 * 2 * P], BF16, name="wgrp", align_bytes=64, bufs=3)
+            regroup(engine_copy, w_bank[(gate, d)], w_grp[(gate, d)], 0)
 
         def quant_w(gate, d):
             codes = const.tile([P, 2 * P], U32, name="wc%d_%d" % (gate, d), align_bytes=64)
@@ -206,25 +210,34 @@ def tile_lstmnetwork_pa_t_kernel(tc, x, w_ih, b_ih, b_hh, out):
                 if c == NCHUNK - 1 and t == RT - 1:
                     nc.sync.dma_start(out=outv[c][:, sl], in_=buf(c, "hid")[:, sl])
 
-        nc.vector.tensor_tensor(out=bsum[0:16, :], in0=bi[:], in1=bh[:], op=ALU.add)
+        low, high = (0, CHUNK // 2), (CHUNK // 2, CHUNK)
         turn_x(0, 0, nc.vector.tensor_copy)
-        turn_x(0, 1, nc.vector.tensor_copy)
-        turn_w(GATE_I, 0, nc.scalar.copy)
-        turn_w(GATE_I, 1, nc.scalar.copy)
-        quant_x(0, 0, CHUNK)
+        turn_w(GATE_I, 0, ring_a, "a")
+        group_w(GATE_I, 0, nc.scalar.copy)
+        nc.vector.tensor_tensor(out=bsum[0:16, :], in0=bi[:], in1=bh[:], op=ALU.add)
+        quant_x(0, *low)
+        turn_w(GATE_I, 1, ring_a, "a")
+        group_w(GATE_I, 1, nc.scalar.copy)
         quant_w(GATE_I, 0)
         bias_ps = ring_v.tile([P, 512], F32, name="bias_ps", tag="v")
         nc.tensor.transpose(bias_ps[:, 0:P], bsum[:], ident[:])
         nc.vector.tensor_copy(out=bias[:], in_=bias_ps[:, 0:16])
         quant_w(GATE_I, 1)
-        turn_w(GATE_G, 0, nc.vector.tensor_copy)
-        turn_w(GATE_G, 1, nc.vector.tensor_copy)
+        turn_x(0, 1, nc.vector.tensor_copy)
         for q in range(NQ):
-            gate_act(0, GATE_I, q, ACT.Sigmoid, "s_i")
+            gate_act(0, GATE_I, q, ACT.Sigmoid, "s_i", *low)
+        quant_x(0, *high)
+        turn_w(GATE_G, 0)
+        turn_w(GATE_G, 1)
+        for q in range(NQ):
+            gate_act(0, GATE_I, q, ACT.Sigmoid, "s_i", *high)
+        group_w(GATE_G, 0, nc.vector.tensor_copy)
+        group_w(GATE_G, 1, nc.vector.tensor_copy)
         quant_w(GATE_G, 0)
         quant_w(GATE_G, 1)
-        turn_w(GATE_O, 0, nc.vector.tensor_copy)
-        turn_w(GATE_O, 1, nc.vector.tensor_copy)
+        for d in range(ND):
+            turn_w(GATE_O, d)
+            group_w(GATE_O, d, nc.vector.tensor_copy)
         quant_w(GATE_O, 0)
         quant_w(GATE_O, 1)
 

@@ -1,5 +1,7 @@
 from contextlib import ExitStack
 
+import math
+
 import concourse.masks as masks
 import concourse.mybir as mybir
 
@@ -26,8 +28,26 @@ LAST_PIECES = 2
 NWARM = 3
 DEPTH = {"s_i": 2, "t_g": 2, "cell": 3, "s_o": 3, "t_c": 3, "hid": 3}
 
+DEG = 8
+VQ = 1
+
 FLOPS = 2 * ROWS * (3 * H * ND) * K
 BYTES = ROWS * K * 2 + ND * 3 * H * K * 2 + 2 * ND * 3 * H * 2 + ROWS * ND * H * 4
+
+
+def tanh_series():
+    nodes = [math.cos(math.pi * (2 * k + 1) / (4 * DEG + 4)) for k in range(DEG + 1)]
+    ys = [v * v for v in nodes]
+    diff = [math.tanh(v) / v for v in nodes]
+    for j in range(1, DEG + 1):
+        for i in range(DEG, j - 1, -1):
+            diff[i] = (diff[i] - diff[i - 1]) / (ys[i] - ys[i - j])
+    poly = [diff[DEG]]
+    for i in range(DEG - 1, -1, -1):
+        shifted = [0.0] + poly
+        poly = [s - ys[i] * p for s, p in zip(shifted, poly + [0.0])]
+        poly[0] += diff[i]
+    return poly
 
 
 def tile_lstmnetwork_pa_t_kernel(tc, x, w_ih, b_ih, b_hh, out):
@@ -181,17 +201,46 @@ def tile_lstmnetwork_pa_t_kernel(tc, x, w_ih, b_ih, b_hh, out):
                 out=buf(c, "cell")[:, sl], in0=buf(c, "s_i")[:, sl], in1=buf(c, "t_g")[:, sl], op=ALU.mult
             )
 
-        def turn_back(pool, tag, src, t):
+        def turn_back(pool, tag, src, t, pairs=NQ):
             bank = pool.tile([P, 512], F32, name="back_" + tag, tag=tag)
-            for q in range(NQ):
+            for q in range(pairs):
                 nc.tensor.transpose(
                     bank[:, q * P : (q + 1) * P], src[:, q * CHUNK + t * P : q * CHUNK + (t + 1) * P], ident[:]
                 )
             return bank
 
+        series = tanh_series()
+        monic = [a / series[DEG] for a in series]
+
+        def scalar_pairs(c, t):
+            return NQ - VQ if c < NCHUNK - 1 and t == RT - 1 else NQ
+
+        def vector_tail(c):
+            def block(tile):
+                return tile[:].rearrange("p (q r) -> p q r", q=NQ)[:, NQ - VQ : NQ, (RT - 1) * P : RT * P]
+
+            cell = block(buf(c, "cell"))
+            s_o = block(buf(c, "s_o"))
+            y = work.tile([P, VQ, P], F32, name="y")
+            u = work.tile([P, VQ, P], F32, name="u")
+
+            def fused(out, in0, scalar, in1, op0):
+                return lambda: nc.vector.scalar_tensor_tensor(
+                    out=out, in0=in0, scalar=scalar, in1=in1, op0=op0, op1=ALU.mult
+                )
+
+            steps = [lambda: nc.vector.tensor_tensor(out=y[:], in0=cell, in1=cell, op=ALU.mult)]
+            steps.append(fused(u[:], y[:], monic[DEG - 1], y[:], ALU.add))
+            for k in range(DEG - 2, 0, -1):
+                steps.append(fused(u[:], u[:], monic[k], y[:], ALU.add))
+            steps.append(fused(u[:], u[:], monic[0], cell, ALU.add))
+            steps.append(fused(s_o, u[:], series[DEG], s_o, ALU.mult))
+            return steps
+
         def cell_tanh(c, t, pieces=1):
-            bank = turn_back(ring_a, "a", buf(c, "cell"), t)
-            w = 512 // pieces
+            pairs = scalar_pairs(c, t)
+            bank = turn_back(ring_a, "a", buf(c, "cell"), t, pairs)
+            w = pairs * P // pieces
             for i in range(pieces):
                 nc.scalar.activation(
                     out=buf(c, "t_c")[:, t * 512 + i * w : t * 512 + (i + 1) * w],
@@ -201,7 +250,11 @@ def tile_lstmnetwork_pa_t_kernel(tc, x, w_ih, b_ih, b_hh, out):
 
         def hidden(c, t, pieces=1):
             bank = turn_back(ring_v, "v", buf(c, "s_o"), t)
-            w = 512 // pieces
+            pairs = scalar_pairs(c, t)
+            if pairs < NQ:
+                ready = slice(t * 512 + pairs * P, (t + 1) * 512)
+                nc.vector.tensor_copy(out=buf(c, "hid")[:, ready], in_=bank[:, pairs * P : 512])
+            w = pairs * P // pieces
             for i in range(pieces):
                 sl = slice(t * 512 + i * w, t * 512 + (i + 1) * w)
                 nc.vector.tensor_tensor(
@@ -244,13 +297,23 @@ def tile_lstmnetwork_pa_t_kernel(tc, x, w_ih, b_ih, b_hh, out):
         def store(c, t0, t1):
             nc.sync.dma_start(out=outv[c][:, t0 * 512 : t1 * 512], in_=buf(c, "hid")[:, t0 * 512 : t1 * 512])
 
+        steps = []
+
+        def step():
+            if steps:
+                first = steps[0]
+                steps.remove(first)
+                first()
+
         for c in range(NCHUNK):
             last = c == NCHUNK - 1
             if c > 0:
+                steps.extend(vector_tail(c - 1))
                 for q in range(NQ):
                     gate_act(c, GATE_I, q, ACT.Sigmoid, "s_i")
             if c >= 2:
                 hidden(c - 2, RT - 1)
+                step()
                 store(c - 2, 0, RT)
             if c == 0:
                 for q in range(NQ):
@@ -258,18 +321,24 @@ def tile_lstmnetwork_pa_t_kernel(tc, x, w_ih, b_ih, b_hh, out):
             if not last:
                 for pair in range(2):
                     turn_x(c + 1, pair, nc.vector.tensor_copy)
+                    step()
             if c > 0:
                 for q in range(NQ):
                     gate_act(c, GATE_G, q, ACT.Tanh, "t_g")
             if not last:
                 quant_x(c + 1, 0, CHUNK)
+                step()
             for q in range(NQ):
                 cell_product(c, q, nc.vector)
+                step()
             if c >= 1:
                 for t in range(RT):
                     cell_tanh(c - 1, t)
                     if t < RT - 1:
                         hidden(c - 1, t)
+                        step()
+            while steps:
+                step()
             for q in range(NQ):
                 gate_act(c, GATE_O, q, ACT.Sigmoid, "s_o")
         c = NCHUNK - 1

@@ -318,16 +318,16 @@ def tile_lstmnetwork_pa_t_kernel(tc, x, w_ih, b_ih, b_hh, out):
             if c == 0:
                 for q in range(NQ):
                     gate_act(c, GATE_G, q, ACT.Tanh, "t_g")
-            if not last:
-                for pair in range(2):
+            for pair in range(2):
+                if not last:
                     turn_x(c + 1, pair, nc.vector.tensor_copy)
-                    step()
+                step()
             if c > 0:
                 for q in range(NQ):
                     gate_act(c, GATE_G, q, ACT.Tanh, "t_g")
             if not last:
                 quant_x(c + 1, 0, CHUNK)
-                step()
+            step()
             for q in range(NQ):
                 cell_product(c, q, nc.vector)
                 step()
@@ -344,9 +344,9 @@ def tile_lstmnetwork_pa_t_kernel(tc, x, w_ih, b_ih, b_hh, out):
         c = NCHUNK - 1
         hidden(c - 1, RT - 1)
         store(c - 1, 0, RT)
-        for t in range(RT):
+        cell_tanh(c, 0)
+        for t in range(1, RT):
             cell_tanh(c, t, LAST_PIECES if t == RT - 1 else 1)
-        for t in range(RT - 1):
-            hidden(c, t)
-            store(c, t, t + 1)
+            hidden(c, t - 1)
+            store(c, t - 1, t)
         hidden(c, RT - 1, LAST_PIECES)

@@ -276,23 +276,24 @@ def tile_lstmnetwork_pa_t_kernel(tc, x, w_ih, b_ih, b_hh, out):
         nc.tensor.transpose(bias_ps[:, 0:P], bsum[:], ident[:])
         nc.vector.tensor_copy(out=bias[:], in_=bias_ps[:, 0:16])
         quant_w(GATE_I, 1)
-        turn_x(0, 1, nc.vector.tensor_copy)
+        turn_x(0, 1, nc.scalar.copy)
+        turn_w(GATE_G, 0)
+        group_w(GATE_G, 0, nc.vector.tensor_copy)
         for q in range(NQ):
             gate_act(0, GATE_I, q, ACT.Sigmoid, "s_i", *low)
         quant_x(0, *high)
-        turn_w(GATE_G, 0)
         turn_w(GATE_G, 1)
+        group_w(GATE_G, 1, nc.vector.tensor_copy)
         for q in range(NQ):
             gate_act(0, GATE_I, q, ACT.Sigmoid, "s_i", *high)
-        group_w(GATE_G, 0, nc.vector.tensor_copy)
-        group_w(GATE_G, 1, nc.vector.tensor_copy)
         quant_w(GATE_G, 0)
         quant_w(GATE_G, 1)
         for d in range(ND):
             turn_w(GATE_O, d)
             group_w(GATE_O, d, nc.vector.tensor_copy)
-        quant_w(GATE_O, 0)
-        quant_w(GATE_O, 1)
+            for h in range(2):
+                gate_act(0, GATE_G, 2 * d + h, ACT.Tanh, "t_g")
+            quant_w(GATE_O, d)
 
         def store(c, t0, t1):
             nc.sync.dma_start(out=outv[c][:, t0 * 512 : t1 * 512], in_=buf(c, "hid")[:, t0 * 512 : t1 * 512])
@@ -315,9 +316,6 @@ def tile_lstmnetwork_pa_t_kernel(tc, x, w_ih, b_ih, b_hh, out):
                 hidden(c - 2, RT - 1)
                 step()
                 store(c - 2, 0, RT)
-            if c == 0:
-                for q in range(NQ):
-                    gate_act(c, GATE_G, q, ACT.Tanh, "t_g")
             for pair in range(2):
                 if not last:
                     turn_x(c + 1, pair, nc.vector.tensor_copy)
@@ -332,19 +330,22 @@ def tile_lstmnetwork_pa_t_kernel(tc, x, w_ih, b_ih, b_hh, out):
                 cell_product(c, q, nc.vector)
                 step()
             if c >= 1:
-                for t in range(RT):
+                for t in range(RT - 1):
                     cell_tanh(c - 1, t)
-                    if t < RT - 1:
-                        hidden(c - 1, t)
-                        step()
+                    hidden(c - 1, t)
+                    step()
+                if not last:
+                    cell_tanh(c - 1, RT - 1)
             while steps:
                 step()
             for q in range(NQ):
                 gate_act(c, GATE_O, q, ACT.Sigmoid, "s_o")
         c = NCHUNK - 1
-        hidden(c - 1, RT - 1)
-        store(c - 1, 0, RT)
+        store(c - 1, 0, RT - 1)
+        cell_tanh(c - 1, RT - 1)
         cell_tanh(c, 0)
+        hidden(c - 1, RT - 1)
+        store(c - 1, RT - 1, RT)
         for t in range(1, RT):
             cell_tanh(c, t, LAST_PIECES if t == RT - 1 else 1)
             hidden(c, t - 1)

@@ -88,8 +88,8 @@ def tile_lstmnetwork_pa_t_kernel(tc, x, w_ih, b_ih, b_hh, out):
         def load_w(gate, d):
             t = const.tile([P, 2 * K], BF16, name="wraw%d_%d" % (gate, d))
             nc.sync.dma_start(
-                out=t[:].rearrange("p (h k) -> p h k", h=2),
-                in_=w_ih[d, gate * H : (gate + 1) * H, :].rearrange("(h p) k -> p h k", p=P),
+                out=t[:],
+                in_=w_ih[d, gate * H : (gate + 1) * H, :].rearrange("(p j) k -> p (j k)", p=P),
             )
             w_raw[(gate, d)] = t
 
@@ -140,7 +140,10 @@ def tile_lstmnetwork_pa_t_kernel(tc, x, w_ih, b_ih, b_hh, out):
 
         def group_w(gate, d, engine_copy):
             w_grp[(gate, d)] = stage.tile([P, 4 * 2 * P], BF16, name="wgrp", align_bytes=64, bufs=3)
-            regroup(engine_copy, w_bank[(gate, d)], w_grp[(gate, d)], 0)
+            engine_copy(
+                out=w_grp[(gate, d)][:].bitcast(F32).rearrange("p (r j u) -> p r j u", j=2, u=2),
+                in_=w_bank[(gate, d)][:].rearrange("p (j u r) -> p r j u", j=2, u=2),
+            )
 
         def quant_w(gate, d):
             codes = const.tile([P, 2 * P], U32, name="wc%d_%d" % (gate, d), align_bytes=64)

from contextlib import ExitStack

import math

import concourse.masks as masks
import concourse.mybir as mybir

F32 = mybir.dt.float32
BF16 = mybir.dt.bfloat16
U32 = mybir.dt.uint32
U8 = mybir.dt.uint8
FP8X4 = mybir.dt.float8_e4m3fn_x4
ACT = mybir.ActivationFunctionType
ALU = mybir.AluOpType

P = 128
ROWS = 4096
K = 512
H = 256
ND = 2
CHUNK = 512
NCHUNK = ROWS // CHUNK
RT = CHUNK // P
NQ = 4
GATE_I, GATE_G, GATE_O = 0, 2, 3
RA, RV = 5, 3
LAST_PIECES = 2
NWARM = 3
DEPTH = {"s_i": 2, "t_g": 2, "cell": 3, "s_o": 3, "t_c": 3, "hid": 3}

DEG = 8
VQ = 1

FLOPS = 2 * ROWS * (3 * H * ND) * K
BYTES = ROWS * K * 2 + ND * 3 * H * K * 2 + 2 * ND * 3 * H * 2 + ROWS * ND * H * 4


def tanh_series():
    nodes = [math.cos(math.pi * (2 * k + 1) / (4 * DEG + 4)) for k in range(DEG + 1)]
    ys = [v * v for v in nodes]
    diff = [math.tanh(v) / v for v in nodes]
    for j in range(1, DEG + 1):
        for i in range(DEG, j - 1, -1):
            diff[i] = (diff[i] - diff[i - 1]) / (ys[i] - ys[i - j])
    poly = [diff[DEG]]
    for i in range(DEG - 1, -1, -1):
        shifted = [0.0] + poly
        poly = [s - ys[i] * p for s, p in zip(shifted, poly + [0.0])]
        poly[0] += diff[i]
    return poly


def tile_lstmnetwork_pa_t_kernel(tc, x, w_ih, b_ih, b_hh, out):
    nc = tc.nc
    xv = x.flatten_outer_dims().rearrange("(c r t) k -> c r (t k)", r=P, t=RT)
    outv = out.rearrange("(c r t) n -> c r (t n)", r=P, t=RT)

    with ExitStack() as ctx:
        ctx.enter_context(tc.manual_schedule())
        const = ctx.enter_context(tc.tile_pool(name="const", bufs=1))
        xin = ctx.enter_context(tc.tile_pool(name="xin", bufs=1))
        stage = ctx.enter_context(tc.tile_pool(name="stage", bufs=2))
        xq = ctx.enter_context(tc.tile_pool(name="xq", bufs=3))
        work = ctx.enter_context(tc.tile_pool(name="work", bufs=2))
        ring_a = ctx.enter_context(tc.psum_pool(name="ring_a", bufs=RA))
        ring_v = ctx.enter_context(tc.psum_pool(name="ring_v", bufs=RV))

        bi = const.tile([16, P], BF16, name="bi")
        bh = const.tile([16, P], BF16, name="bh")
        nc.scalar.dma_start(out=bi[:], in_=b_ih.rearrange("d (g p) -> (d g) p", p=P))
        nc.scalar.dma_start(out=bh[:], in_=b_hh.rearrange("d (g p) -> (d g) p", p=P))
        zeros = const.tile([P, 512], BF16, name="zeros")
        nc.vector.memset(zeros[:], 0.0)
        spin = ring_a.tile([P, 512], F32, name="spin", tag="a")
        for i in range(NWARM):
            nc.tensor.matmul(out=spin[:], lhsT=zeros[:, 0:P], rhs=zeros[:], start=True, stop=True)
        warm = const.tile([P, 1], F32, name="warm")
        nc.vector.memset(warm[:], 0.0)
        nc.scalar.activation(out=warm[:], in_=warm[:], func=ACT.Sigmoid)
        ident = const.tile([P, P], F32, name="ident")
        masks.make_identity(nc, ident[:])
        bsum = const.tile([P, P], F32, name="bsum")
        nc.vector.memset(bsum[:], 0.0)

        w_raw = {}
        x_raw = {}

        def load_w(gate, d):
            t = const.tile([P, 2 * K], BF16, name="wraw%d_%d" % (gate, d))
            nc.sync.dma_start(
                out=t[:],
                in_=w_ih[d, gate * H : (gate + 1) * H, :].rearrange("(p j) k -> p (j k)", p=P),
            )
            w_raw[(gate, d)] = t

        def load_x(c):
            x_raw[c] = xin.tile([P, RT * K], BF16, name="xraw%d" % c)
            nc.sync.dma_start(out=x_raw[c][:], in_=xv[c])

        x_raw[0] = xin.tile([P, RT * K], BF16, name="xraw0")
        half = RT * K // 2
        nc.sync.dma_start(out=x_raw[0][:, 0:half], in_=xv[0][:, 0:half])
        load_w(GATE_I, 0)
        load_w(GATE_I, 1)
        nc.sync.dma_start(out=x_raw[0][:, half : 2 * half], in_=xv[0][:, half : 2 * half])
        load_w(GATE_G, 0)
        load_w(GATE_G, 1)
        load_w(GATE_O, 0)
        load_w(GATE_O, 1)
        for c in range(1, NCHUNK):
            load_x(c)

        def turn(raw, first, pool=ring_v, tag="v"):
            raw32 = raw[:].bitcast(F32)
            bank = pool.tile([P, 512], F32, name="turn_" + tag, tag=tag)
            for j in range(2):
                for u in range(2):
                    nc.tensor.transpose(
                        bank[:, (2 * j + u) * P : (2 * j + u + 1) * P],
                        raw32[:, (first + j) * 256 + u : (first + j + 1) * 256 : 2],
                        ident[:],
                    )
            return bank

        def regroup(engine_copy, bank, grouped, pair):
            g32 = grouped[:].bitcast(F32)
            engine_copy(
                out=g32[:, pair * 512 : (pair + 1) * 512].rearrange("p (j r u) -> p j r u", j=2, u=2),
                in_=bank[:].rearrange("p (j u r) -> p j r u", j=2, u=2),
            )

        w_grp = {}
        w_codes = {}
        w_scales = {}

        w_bank = {}

        def turn_w(gate, d, pool=ring_v, tag="v"):
            w_bank[(gate, d)] = turn(w_raw[(gate, d)], 0, pool, tag)

        def group_w(gate, d, engine_copy):
            w_grp[(gate, d)] = stage.tile([P, 4 * 2 * P], BF16, name="wgrp", align_bytes=64, bufs=3)
            engine_copy(
                out=w_grp[(gate, d)][:].bitcast(F32).rearrange("p (r j u) -> p r j u", j=2, u=2),
                in_=w_bank[(gate, d)][:].rearrange("p (j u r) -> p r j u", j=2, u=2),
            )

        def quant_w(gate, d):
            codes = const.tile([P, 2 * P], U32, name="wc%d_%d" % (gate, d), align_bytes=64)
            scales = const.tile([P, 2 * P], U8, name="ws%d_%d" % (gate, d), align_bytes=64)
            nc.vector.quantize_mx(out=codes[:].bitcast(FP8X4), scales=scales[:], in_=w_grp[(gate, d)][:])
            w_codes[(gate, d)] = codes
            w_scales[(gate, d)] = scales

        x_grp = {}
        x_codes = {}
        x_scales = {}

        def turn_x(c, pair, engine_copy):
            if pair == 0:
                x_grp[c] = stage.tile([P, 4 * CHUNK], BF16, name="xgrp", align_bytes=64)
            regroup(engine_copy, turn(x_raw[c], 2 * pair), x_grp[c], pair)

        def quant_x(c, lo, hi):
            if c not in x_codes:
                x_codes[c] = xq.tile([P, CHUNK], U32, name="xc", align_bytes=64)
                x_scales[c] = xq.tile([P, CHUNK], U8, name="xs", align_bytes=64)
            nc.vector.quantize_mx(
                out=x_codes[c][:, lo:hi].bitcast(FP8X4), scales=x_scales[c][:, lo:hi], in_=x_grp[c][:, 4 * lo : 4 * hi]
            )

        bias = const.tile([P, 16], F32, name="bias")
        tiles = {}

        def buf(c, name):
            if (c, name) not in tiles:
                tiles[(c, name)] = work.tile([P, NQ * CHUNK], F32, name=name, bufs=DEPTH[name])
            return tiles[(c, name)]

        def gate_act(c, gate, q, func, name, lo=0, hi=CHUNK):
            d, h = divmod(q, 2)
            acc = ring_a.tile([P, hi - lo], F32, name="acc", tag="a")
            nc.tensor.matmul_mx(
                out=acc[:],
                lhsT=w_codes[(gate, d)][:, h * P : (h + 1) * P].bitcast(FP8X4),
                lhsT_scale=w_scales[(gate, d)][:, h * P : (h + 1) * P],
                rhs=x_codes[c][:, lo:hi].bitcast(FP8X4),
                rhs_scale=x_scales[c][:, lo:hi],
                start=True,
                stop=True,
            )
            col = d * 8 + gate * 2 + h
            nc.scalar.activation(
                out=buf(c, name)[:, q * CHUNK + lo : q * CHUNK + hi],
                in_=acc[:],
                func=func,
                bias=bias[:, col : col + 1],
                scale=1.0,
            )

        def cell_product(c, q, engine):
            sl = slice(q * CHUNK, (q + 1) * CHUNK)
            engine.tensor_tensor(
                out=buf(c, "cell")[:, sl], in0=buf(c, "s_i")[:, sl], in1=buf(c, "t_g")[:, sl], op=ALU.mult
            )

        def turn_back(pool, tag, src, t, pairs=NQ):
            bank = pool.tile([P, 512], F32, name="back_" + tag, tag=tag)
            for q in range(pairs):
                nc.tensor.transpose(
                    bank[:, q * P : (q + 1) * P], src[:, q * CHUNK + t * P : q * CHUNK + (t + 1) * P], ident[:]
                )
            return bank

        series = tanh_series()
        monic = [a / series[DEG] for a in series]

        def scalar_pairs(c, t):
            return NQ - VQ if c < NCHUNK - 1 and t == RT - 1 else NQ

        def vector_tail(c):
            def block(tile):
                return tile[:].rearrange("p (q r) -> p q r", q=NQ)[:, NQ - VQ : NQ, (RT - 1) * P : RT * P]

            cell = block(buf(c, "cell"))
            s_o = block(buf(c, "s_o"))
            y = work.tile([P, VQ, P], F32, name="y")
            u = work.tile([P, VQ, P], F32, name="u")

            def fused(out, in0, scalar, in1, op0):
                return lambda: nc.vector.scalar_tensor_tensor(
                    out=out, in0=in0, scalar=scalar, in1=in1, op0=op0, op1=ALU.mult
                )

            steps = [lambda: nc.vector.tensor_tensor(out=y[:], in0=cell, in1=cell, op=ALU.mult)]
            steps.append(fused(u[:], y[:], monic[DEG - 1], y[:], ALU.add))
            for k in range(DEG - 2, 0, -1):
                steps.append(fused(u[:], u[:], monic[k], y[:], ALU.add))
            steps.append(fused(u[:], u[:], monic[0], cell, ALU.add))
            steps.append(fused(s_o, u[:], series[DEG], s_o, ALU.mult))
            return steps

        def cell_tanh(c, t, pieces=1):
            pairs = scalar_pairs(c, t)
            bank = turn_back(ring_a, "a", buf(c, "cell"), t, pairs)
            w = pairs * P // pieces
            for i in range(pieces):
                nc.scalar.activation(
                    out=buf(c, "t_c")[:, t * 512 + i * w : t * 512 + (i + 1) * w],
                    in_=bank[:, i * w : (i + 1) * w],
                    func=ACT.Tanh,
                )

        def hidden(c, t, pieces=1):
            bank = turn_back(ring_v, "v", buf(c, "s_o"), t)
            pairs = scalar_pairs(c, t)
            if pairs < NQ:
                ready = slice(t * 512 + pairs * P, (t + 1) * 512)
                nc.vector.tensor_copy(out=buf(c, "hid")[:, ready], in_=bank[:, pairs * P : 512])
            w = pairs * P // pieces
            for i in range(pieces):
                sl = slice(t * 512 + i * w, t * 512 + (i + 1) * w)
                nc.vector.tensor_tensor(
                    out=buf(c, "hid")[:, sl], in0=bank[:, i * w : (i + 1) * w], in1=buf(c, "t_c")[:, sl], op=ALU.mult
                )
                if c == NCHUNK - 1 and t == RT - 1:
                    nc.sync.dma_start(out=outv[c][:, sl], in_=buf(c, "hid")[:, sl])

        low, high = (0, CHUNK // 2), (CHUNK // 2, CHUNK)
        turn_x(0, 0, nc.vector.tensor_copy)
        turn_w(GATE_I, 0, ring_a, "a")
        group_w(GATE_I, 0, nc.scalar.copy)
        nc.vector.tensor_tensor(out=bsum[0:16, :], in0=bi[:], in1=bh[:], op=ALU.add)
        quant_x(0, *low)
        turn_w(GATE_I, 1, ring_a, "a")
        group_w(GATE_I, 1, nc.scalar.copy)
        quant_w(GATE_I, 0)
        bias_ps = ring_v.tile([P, 512], F32, name="bias_ps", tag="v")
        nc.tensor.transpose(bias_ps[:, 0:P], bsum[:], ident[:])
        nc.vector.tensor_copy(out=bias[:], in_=bias_ps[:, 0:16])
        quant_w(GATE_I, 1)
        turn_x(0, 1, nc.scalar.copy)
        turn_w(GATE_G, 0)
        group_w(GATE_G, 0, nc.vector.tensor_copy)
        for q in range(NQ):
            gate_act(0, GATE_I, q, ACT.Sigmoid, "s_i", *low)
        quant_x(0, *high)
        turn_w(GATE_G, 1)
        group_w(GATE_G, 1, nc.vector.tensor_copy)
        for q in range(NQ):
            gate_act(0, GATE_I, q, ACT.Sigmoid, "s_i", *high)
        quant_w(GATE_G, 0)
        quant_w(GATE_G, 1)
        for d in range(ND):
            turn_w(GATE_O, d)
            group_w(GATE_O, d, nc.vector.tensor_copy)
            for h in range(2):
                gate_act(0, GATE_G, 2 * d + h, ACT.Tanh, "t_g")
            quant_w(GATE_O, d)

        def store(c, t0, t1):
            nc.sync.dma_start(out=outv[c][:, t0 * 512 : t1 * 512], in_=buf(c, "hid")[:, t0 * 512 : t1 * 512])

        steps = []

        def step():
            if steps:
                first = steps[0]
                steps.remove(first)
                first()

        for c in range(NCHUNK):
            last = c == NCHUNK - 1
            if c > 0:
                steps.extend(vector_tail(c - 1))
                for q in range(NQ):
                    gate_act(c, GATE_I, q, ACT.Sigmoid, "s_i")
            if c >= 2:
                hidden(c - 2, RT - 1)
                step()
                store(c - 2, 0, RT)
            for pair in range(2):
                if not last:
                    turn_x(c + 1, pair, nc.vector.tensor_copy)
                step()
            if c > 0:
                for q in range(NQ):
                    gate_act(c, GATE_G, q, ACT.Tanh, "t_g")
            if not last:
                quant_x(c + 1, 0, CHUNK)
            step()
            for q in range(NQ):
                cell_product(c, q, nc.vector)
                step()
            if c >= 1:
                for t in range(RT - 1):
                    cell_tanh(c - 1, t)
                    hidden(c - 1, t)
                    step()
                if not last:
                    cell_tanh(c - 1, RT - 1)
            while steps:
                step()
            for q in range(NQ):
                gate_act(c, GATE_O, q, ACT.Sigmoid, "s_o")
        c = NCHUNK - 1
        store(c - 1, 0, RT - 1)
        cell_tanh(c - 1, RT - 1)
        cell_tanh(c, 0)
        hidden(c - 1, RT - 1)
        store(c - 1, RT - 1, RT)
        for t in range(1, RT):
            cell_tanh(c, t, LAST_PIECES if t == RT - 1 else 1)
            hidden(c, t - 1)
            store(c, t - 1, t)
        hidden(c, RT - 1, LAST_PIECES)
